import numpy as np
import ml_dtypes


def mxq(x, axis, fmt="e4m3"):
    dtype, down = {"e4m3": (ml_dtypes.float8_e4m3fn, 7), "e5m2": (ml_dtypes.float8_e5m2, 14)}[fmt]
    v = np.moveaxis(np.asarray(x, np.float32).astype(ml_dtypes.bfloat16).astype(np.float64), axis, -1)
    blocks = v.reshape(v.shape[:-1] + (-1, 32))
    amax = np.abs(blocks).max(-1, keepdims=True)
    byte = np.maximum(np.where(amax > 0, np.frexp(amax)[1] - 1 + 127, 0) - down, 1)
    scale = np.exp2(byte - 127.0)
    codes = (blocks / scale).astype(np.float32).astype(dtype).astype(np.float64)
    return np.moveaxis((codes * scale).reshape(v.shape), -1, axis)


WIDE = False


def mx_kscale(k):
    if not WIDE:
        return np.ones(k)
    levels = np.array([10, -10, 5, -5, 0])
    a = np.random.permutation(np.resize(levels, k // 512 * 4)).reshape(k // 512, 4)
    idx = np.arange(k)
    return np.exp2(a[idx // 512, idx % 128 // 32])


BF16 = ml_dtypes.bfloat16


def bf(x):
    return np.asarray(x, np.float32).astype(BF16)


def f64(x):
    return np.asarray(x).astype(np.float64)


E2M1 = np.array([0.0, 0.5, 1.0, 1.5, 2.0, 3.0, 4.0, 6.0, -0.0, -0.5, -1.0, -1.5, -2.0, -3.0, -4.0, -6.0])


def pack_weight(w, fmt):
    k, n = w.shape
    w = f64(bf(w)).reshape(k // 32, 32, n)
    amax = np.abs(w).max(1)
    if fmt == "e4m3":
        byte = np.frexp(amax)[1] - 1 + 127 - 7
    else:
        mant, ex = np.frexp(amax / 6.0)
        byte = np.where(mant > 0.5, ex, ex - 1) + 127
    byte = np.clip(np.where(amax > 0, byte, 1), 1, 254)
    scaled = (w * np.exp2(127.0 - byte)[:, None, :]).reshape(k, n).astype(np.float32)
    by_word = np.ascontiguousarray(scaled.reshape(k // 512, 128, 4, n).transpose(0, 1, 3, 2))
    if fmt == "e4m3":
        words = by_word.astype(ml_dtypes.float8_e4m3fn).view(np.uint8)
    else:
        c = by_word.astype(ml_dtypes.float4_e2m1fn).view(np.uint8) & 0xF
        words = c[..., 0::2] | (c[..., 1::2] << 4)
    return np.ascontiguousarray(words), np.ascontiguousarray(byte.astype(np.uint8).reshape(k // 512, 16, n))


def unpack_weight(words, scales, fmt):
    g, p, n, _ = words.shape
    if fmt == "e4m3":
        vals = np.ascontiguousarray(words).view(ml_dtypes.float8_e4m3fn).astype(np.float64)
    else:
        nib = np.empty((g, p, n, 4), np.uint8)
        nib[..., 0::2] = words & 0xF
        nib[..., 1::2] = words >> 4
        vals = E2M1[nib]
    vals = vals * np.repeat(np.exp2(scales.astype(np.float64) - 127.0), 8, axis=1)[..., None]
    return vals.transpose(0, 1, 3, 2).reshape(g * 512, n)


BS, D, R = 128, 16384, 1024
ALPHA = 1.0


def setup_inputs():
    s = mx_kscale(D)
    f = np.random.standard_normal((BS, D)) + np.random.standard_normal((BS, 1)) * np.random.standard_normal((1, D))
    features = bf(f * s)
    words, scales = pack_weight(np.random.standard_normal((D, R)) * np.sqrt(0.5 / (D * R)) / s[:, None], "e4m3")
    return {"features": features, "P_words": words, "P_scales": scales}


def reference(features, P_words, P_scales):
    Z = mxq(f64(features), 1, "e4m3") @ unpack_weight(P_words, P_scales, "e4m3")
    sq_norm = np.sum(Z * Z, axis=1)
    Zq = mxq(Z, 1, "e4m3")
    sq = sq_norm[:, None] + sq_norm[None, :] - 2.0 * (Zq @ Zq.T)
    sq = np.maximum(sq, 0.0)
    eye = np.eye(Z.shape[0], dtype=bool)
    dist = np.where(eye, 0.0, np.sqrt(np.where(eye, 1.0, sq)))
    adjacency_pre = np.exp(-ALPHA * dist)
    d_inv_sqrt = 1.0 / np.sqrt(np.sum(adjacency_pre, axis=1))
    normalized = d_inv_sqrt[:, None] * adjacency_pre * d_inv_sqrt[None, :]
    return (normalized, adjacency_pre)

@@ -1,0 +1,188 @@
+from contextlib import ExitStack
+
+import concourse.mybir as mybir
+from concourse.masks import make_identity
+
+F32 = mybir.dt.float32
+BF16 = mybir.dt.bfloat16
+I32 = mybir.dt.int32
+U32 = mybir.dt.uint32
+U8 = mybir.dt.uint8
+FP8X4 = mybir.dt.float8_e4m3fn_x4
+ALU = mybir.AluOpType
+ACT = mybir.ActivationFunctionType
+
+P = 128
+PACK = 4
+K_PASS = P * PACK
+D = 16384
+R = 1024
+GROUPS = D // K_PASS
+N_TILE = 512
+HALVES = R // N_TILE
+PLANES = 4
+GROUPS_PER_X_LOAD = 8
+GROUPS_PER_W_LOAD = 2
+GROUPS_PER_BANK = 2
+
+SQ_MIN = 2.0 ** -100
+SQ_MAX = 2.0 ** 118
+
+FLOPS = 2 * P * D * R + 2 * P * P * R
+
+
+def tile_metric_learning_based_adjacency_matrix_k_kernel(tc, features, P_words, P_scales, out_0, out_1):
+    nc = tc.nc
+    with ExitStack() as ctx:
+        keep = ctx.enter_context(tc.tile_pool(name="keep", bufs=1))
+        stage = ctx.enter_context(tc.tile_pool(name="stage", bufs=4))
+        psum_z = ctx.enter_context(tc.psum_pool(name="psum_z", bufs=1))
+
+        x_loads = []
+        for c in range(GROUPS // GROUPS_PER_X_LOAD):
+            x_sb = keep.tile([P, GROUPS_PER_X_LOAD * K_PASS], BF16, name="x%d" % c)
+            width = GROUPS_PER_X_LOAD * K_PASS
+            nc.sync.dma_start(out=x_sb[:], in_=features[:, c * width : (c + 1) * width])
+            x_loads.append(x_sb)
+
+        w_planes = keep.tile([P, (GROUPS // PLANES) * R], U8, align_bytes=64)
+        nc.vector.memset(w_planes[:].bitcast(I32), 0)
+        for a in range(GROUPS // PLANES):
+            for q in range(4):
+                nc.sync.dma_start(
+                    out=w_planes[32 * q : 32 * q + 16, a * R : (a + 1) * R].bitcast(I32),
+                    in_=P_scales[PLANES * a : PLANES * (a + 1), 4 * q : 4 * q + 4, :].bitcast(I32),
+                )
+
+        w_loads = []
+        for c in range(GROUPS // GROUPS_PER_W_LOAD):
+            w_sb = keep.tile([P, GROUPS_PER_W_LOAD, R], U32, name="w%d" % c, align_bytes=64)
+            g0 = c * GROUPS_PER_W_LOAD
+            nc.sync.dma_start(
+                out=w_sb[:].bitcast(I32),
+                in_=P_words[g0 : g0 + GROUPS_PER_W_LOAD].rearrange("g p n t -> p g (n t)").bitcast(I32),
+            )
+            w_loads.append(w_sb)
+
+        ident_f32 = keep.tile([P, P], F32)
+        make_identity(nc, ident_f32[:])
+        ident_bf16 = keep.tile([P, P], BF16)
+        make_identity(nc, ident_bf16[:])
+        off_diagonal = keep.tile([P, P], F32)
+        nc.vector.tensor_scalar(
+            out=off_diagonal[:], in0=ident_f32[:], scalar1=-1.0, scalar2=1.0, op0=ALU.mult, op1=ALU.add
+        )
+        minus_half = keep.tile([P, 1], F32)
+        nc.gpsimd.memset(minus_half[:], -0.5)
+        one = keep.tile([P, 1], F32)
+        nc.gpsimd.memset(one[:], 1.0)
+        sqrt_of_one = keep.tile([P, 1], F32)
+        nc.scalar.activation(out=sqrt_of_one[:], in_=one[:], func=ACT.Sqrt)
+
+        x_codes = keep.tile([P, GROUPS * P], U32, align_bytes=64)
+        x_scales = keep.tile([P, GROUPS * P], U8, align_bytes=64)
+        with tc.psum_pool(name="psum_x", bufs=4) as psum_x:
+            for bank in range(GROUPS // GROUPS_PER_BANK):
+                xt = psum_x.tile([P, GROUPS_PER_BANK, 2, P], F32)
+                for j in range(GROUPS_PER_BANK):
+                    g = bank * GROUPS_PER_BANK + j
+                    x_words = x_loads[g // GROUPS_PER_X_LOAD][:].bitcast(F32)
+                    first = (g % GROUPS_PER_X_LOAD) * (K_PASS // 2)
+                    for u in range(2):
+                        nc.tensor.transpose(
+                            out=xt[:, j, u, :],
+                            in_=x_words[:, first + u : first + K_PASS // 2 : 2],
+                            identity=ident_f32[:],
+                        )
+                grouped = stage.tile([P, GROUPS_PER_BANK * K_PASS], BF16, align_bytes=64)
+                nc.scalar.copy(
+                    out=grouped[:].bitcast(F32).rearrange("p (j i u) -> p j i u", j=GROUPS_PER_BANK, u=2),
+                    in_=xt[:].rearrange("p j u i -> p j i u"),
+                )
+                cols = slice(bank * GROUPS_PER_BANK * P, (bank + 1) * GROUPS_PER_BANK * P)
+                nc.vector.quantize_mx(out=x_codes[:, cols].bitcast(FP8X4), scales=x_scales[:, cols], in_=grouped[:])
+
+        z_banks = [psum_z.tile([P, N_TILE], F32, name="z%d" % h) for h in range(HALVES)]
+        for g in range(GROUPS):
+            w_sb = w_loads[g // GROUPS_PER_W_LOAD]
+            a, b = divmod(g, PLANES)
+            for h in range(HALVES):
+                nc.tensor.matmul_mx(
+                    out=z_banks[h][:],
+                    lhsT=x_codes[:, g * P : (g + 1) * P].bitcast(FP8X4),
+                    lhsT_scale=x_scales[:, g * P : (g + 1) * P],
+                    rhs=w_sb[:, g % GROUPS_PER_W_LOAD, h * N_TILE : (h + 1) * N_TILE].bitcast(FP8X4),
+                    rhs_scale=w_planes[4 * b : P, a * R + h * N_TILE : a * R + (h + 1) * N_TILE],
+                    start=(g == 0),
+                    stop=(g == GROUPS - 1),
+                )
+
+        psum_tail = ctx.enter_context(tc.psum_pool(name="psum_tail", bufs=1))
+
+        n_halves = keep.tile([P, HALVES], F32)
+        z_codes = keep.tile([P, HALVES * P], U32, align_bytes=64)
+        z_scales = keep.tile([P, HALVES * P], U8, align_bytes=64)
+        gram = psum_tail.tile([P, P], F32)
+        for h in range(HALVES):
+            z_sorted = keep.tile([P, PACK, P], BF16, name="z_sorted%d" % h)
+            nc.vector.tensor_copy(out=z_sorted[:], in_=z_banks[h][:].rearrange("i (p t) -> i t p", t=PACK))
+            z_squared = keep.tile([P, N_TILE], F32, name="z_squared%d" % h)
+            nc.scalar.activation(
+                out=z_squared[:], in_=z_banks[h][:], func=ACT.Square, accum_out=n_halves[:, h : h + 1]
+            )
+            zt = psum_tail.tile([P, PACK, P], BF16, name="zt%d" % h)
+            for t in range(PACK):
+                nc.tensor.transpose(out=zt[:, t, :], in_=z_sorted[:, t, :], identity=ident_bf16[:])
+            z_grouped = keep.tile([P, P, PACK], BF16, name="z_grouped%d" % h, align_bytes=64)
+            nc.vector.tensor_copy(out=z_grouped[:], in_=zt[:].rearrange("p t i -> p i t"))
+            nc.vector.quantize_mx(
+                out=z_codes[:, h * P : (h + 1) * P].bitcast(FP8X4),
+                scales=z_scales[:, h * P : (h + 1) * P],
+                in_=z_grouped[:].rearrange("p i t -> p (i t)"),
+            )
+        for h in range(HALVES):
+            nc.tensor.matmul_mx(
+                out=gram[:],
+                lhsT=z_codes[:, h * P : (h + 1) * P].bitcast(FP8X4),
+                lhsT_scale=z_scales[:, h * P : (h + 1) * P],
+                rhs=z_codes[:, h * P : (h + 1) * P].bitcast(FP8X4),
+                rhs_scale=z_scales[:, h * P : (h + 1) * P],
+                start=(h == 0),
+                stop=(h == HALVES - 1),
+            )
+
+        n = keep.tile([P, 1], F32)
+        nc.vector.tensor_add(out=n[:], in0=n_halves[:, 0:1], in1=n_halves[:, 1:2])
+        n_row = psum_tail.tile([P, P], F32)
+        nc.tensor.matmul(out=n_row[:], lhsT=n[:, 0:1].to_broadcast([P, P]), rhs=ident_f32[:], start=True, stop=True)
+        n_sum = keep.tile([P, P], F32)
+        nc.vector.tensor_scalar(out=n_sum[:], in0=n_row[:], scalar1=n[:, 0:1], scalar2=None, op0=ALU.add)
+
+        sq = keep.tile([P, P], F32)
+        nc.vector.scalar_tensor_tensor(
+            out=sq[:], in0=gram[:], scalar=-2.0, in1=n_sum[:], op0=ALU.mult, op1=ALU.add
+        )
+        sq_clamped = keep.tile([P, P], F32)
+        nc.vector.tensor_scalar(
+            out=sq_clamped[:], in0=sq[:], scalar1=SQ_MIN, scalar2=SQ_MAX, op0=ALU.max, op1=ALU.min
+        )
+        root = keep.tile([P, P], F32)
+        nc.scalar.activation(out=root[:], in_=sq_clamped[:], func=ACT.Sqrt)
+        dist = keep.tile([P, P], F32)
+        nc.vector.tensor_mul(out=dist[:], in0=root[:], in1=off_diagonal[:])
+        adjacency = keep.tile([P, P], F32)
+        deg = keep.tile([P, 1], F32)
+        nc.scalar.activation(out=adjacency[:], in_=dist[:], func=ACT.Exp, scale=-1.0, accum_out=deg[:])
+        nc.sync.dma_start(out=out_1[:, :], in_=adjacency[:])
+
+        inv_sqrt_deg = keep.tile([P, 1], F32)
+        nc.gpsimd.tensor_tensor(out=inv_sqrt_deg[:], in0=deg[:], in1=minus_half[:], op=ALU.pow)
+        inv_row = psum_tail.tile([P, P], F32)
+        nc.tensor.matmul(
+            out=inv_row[:], lhsT=inv_sqrt_deg[:, 0:1].to_broadcast([P, P]), rhs=ident_f32[:], start=True, stop=True
+        )
+        normalized = keep.tile([P, P], F32)
+        nc.vector.scalar_tensor_tensor(
+            out=normalized[:], in0=adjacency[:], scalar=inv_sqrt_deg[:, 0:1], in1=inv_row[:], op0=ALU.mult, op1=ALU.mult
+        )
+        nc.sync.dma_start(out=out_0[:, :], in_=normalized[:])

@@ -47,11 +47,12 @@ def tile_metric_learning_based_adjacency_matrix_k_kernel(tc, features, P_words, 
 
         w_planes = keep.tile([P, (GROUPS // PLANES) * R], U8, align_bytes=64)
         nc.vector.memset(w_planes[:].bitcast(I32), 0)
-        for a in range(GROUPS // PLANES):
-            for q in range(4):
-                nc.sync.dma_start(
-                    out=w_planes[32 * q : 32 * q + 16, a * R : (a + 1) * R].bitcast(I32),
-                    in_=P_scales[PLANES * a : PLANES * (a + 1), 4 * q : 4 * q + 4, :].bitcast(I32),
+        scale_rows = P_scales.rearrange("(a b) (q r) n -> q r b a n", b=PLANES, r=4)
+        for q in range(4):
+            for r in range(4):
+                nc.gpsimd.dma_start(
+                    out=w_planes[32 * q + r : 32 * q + 16 : 4, :].rearrange("b (a n) -> b a n", n=R).bitcast(F32),
+                    in_=scale_rows[q, r].bitcast(F32),
                 )
 
         w_loads = []

@@ -24,6 +24,8 @@ PLANES = 4
 GROUPS_PER_X_LOAD = 8
 GROUPS_PER_W_LOAD = 2
 GROUPS_PER_BANK = 2
+SPLIT_GROUPS = 4
+WHOLE_GROUPS = GROUPS - SPLIT_GROUPS
 
 SQ_MIN = 2.0 ** -100
 SQ_MAX = 2.0 ** 118
@@ -47,23 +49,36 @@ def tile_metric_learning_based_adjacency_matrix_k_kernel(tc, features, P_words, 
 
         w_planes = keep.tile([P, (GROUPS // PLANES) * R], U8, align_bytes=64)
         nc.vector.memset(w_planes[:].bitcast(I32), 0)
-        scale_rows = P_scales.rearrange("(a b) (q r) n -> q r b a n", b=PLANES, r=4)
-        for q in range(4):
-            for r in range(4):
-                nc.gpsimd.dma_start(
-                    out=w_planes[32 * q + r : 32 * q + 16 : 4, :].rearrange("b (a n) -> b a n", n=R).bitcast(F32),
-                    in_=scale_rows[q, r].bitcast(F32),
+        for a in range(GROUPS // PLANES):
+            for q in range(4):
+                nc.sync.dma_start(
+                    out=w_planes[32 * q : 32 * q + 16, a * R : (a + 1) * R].bitcast(I32),
+                    in_=P_scales[PLANES * a : PLANES * (a + 1), 4 * q : 4 * q + 4, :].bitcast(I32),
                 )
 
-        w_loads = []
-        for c in range(GROUPS // GROUPS_PER_W_LOAD):
-            w_sb = keep.tile([P, GROUPS_PER_W_LOAD, R], U32, name="w%d" % c, align_bytes=64)
-            g0 = c * GROUPS_PER_W_LOAD
+        w_words = {}
+        for g0 in range(0, WHOLE_GROUPS, GROUPS_PER_W_LOAD):
+            w_sb = keep.tile([P, GROUPS_PER_W_LOAD, R], U32, name="w%d" % g0, align_bytes=64)
             nc.sync.dma_start(
                 out=w_sb[:].bitcast(I32),
                 in_=P_words[g0 : g0 + GROUPS_PER_W_LOAD].rearrange("g p n t -> p g (n t)").bitcast(I32),
             )
-            w_loads.append(w_sb)
+            for j in range(GROUPS_PER_W_LOAD):
+                for h in range(HALVES):
+                    w_words[(g0 + j, h)] = w_sb[:, j, h * N_TILE : (h + 1) * N_TILE]
+        w_first = keep.tile([P, SPLIT_GROUPS, N_TILE], U32, align_bytes=64)
+        nc.sync.dma_start(
+            out=w_first[:].bitcast(I32),
+            in_=P_words[WHOLE_GROUPS:GROUPS, :, 0:N_TILE, :].rearrange("g p n t -> p g (n t)").bitcast(I32),
+        )
+        for g in range(WHOLE_GROUPS, GROUPS):
+            w_words[(g, 0)] = w_first[:, g - WHOLE_GROUPS, :]
+            w_second = keep.tile([P, N_TILE], U32, name="w_second%d" % g, align_bytes=64)
+            nc.sync.dma_start(
+                out=w_second[:].bitcast(I32),
+                in_=P_words[g, :, N_TILE:R, :].rearrange("p n t -> p (n t)").bitcast(I32),
+            )
+            w_words[(g, 1)] = w_second[:]
 
         ident_f32 = keep.tile([P, P], F32)
         make_identity(nc, ident_f32[:])
@@ -104,27 +119,27 @@ def tile_metric_learning_based_adjacency_matrix_k_kernel(tc, features, P_words, 
                 nc.vector.quantize_mx(out=x_codes[:, cols].bitcast(FP8X4), scales=x_scales[:, cols], in_=grouped[:])
 
         z_banks = [psum_z.tile([P, N_TILE], F32, name="z%d" % h) for h in range(HALVES)]
-        for g in range(GROUPS):
-            w_sb = w_loads[g // GROUPS_PER_W_LOAD]
+
+        def z_pass(g, h):
             a, b = divmod(g, PLANES)
-            for h in range(HALVES):
-                nc.tensor.matmul_mx(
-                    out=z_banks[h][:],
-                    lhsT=x_codes[:, g * P : (g + 1) * P].bitcast(FP8X4),
-                    lhsT_scale=x_scales[:, g * P : (g + 1) * P],
-                    rhs=w_sb[:, g % GROUPS_PER_W_LOAD, h * N_TILE : (h + 1) * N_TILE].bitcast(FP8X4),
-                    rhs_scale=w_planes[4 * b : P, a * R + h * N_TILE : a * R + (h + 1) * N_TILE],
-                    start=(g == 0),
-                    stop=(g == GROUPS - 1),
-                )
+            nc.tensor.matmul_mx(
+                out=z_banks[h][:],
+                lhsT=x_codes[:, g * P : (g + 1) * P].bitcast(FP8X4),
+                lhsT_scale=x_scales[:, g * P : (g + 1) * P],
+                rhs=w_words[(g, h)].bitcast(FP8X4),
+                rhs_scale=w_planes[4 * b : P, a * R + h * N_TILE : a * R + (h + 1) * N_TILE],
+                start=(g == 0),
+                stop=(g == GROUPS - 1),
+            )
 
         psum_tail = ctx.enter_context(tc.psum_pool(name="psum_tail", bufs=1))
-
         n_halves = keep.tile([P, HALVES], F32)
         z_codes = keep.tile([P, HALVES * P], U32, align_bytes=64)
         z_scales = keep.tile([P, HALVES * P], U8, align_bytes=64)
         gram = psum_tail.tile([P, P], F32)
-        for h in range(HALVES):
+        n_row = psum_tail.tile([P, P], F32)
+
+        def finish_bank(h):
             z_sorted = keep.tile([P, PACK, P], BF16, name="z_sorted%d" % h)
             nc.vector.tensor_copy(out=z_sorted[:], in_=z_banks[h][:].rearrange("i (p t) -> i t p", t=PACK))
             z_squared = keep.tile([P, N_TILE], F32, name="z_squared%d" % h)
@@ -134,30 +149,46 @@ def tile_metric_learning_based_adjacency_matrix_k_kernel(tc, features, P_words, 
             zt = psum_tail.tile([P, PACK, P], BF16, name="zt%d" % h)
             for t in range(PACK):
                 nc.tensor.transpose(out=zt[:, t, :], in_=z_sorted[:, t, :], identity=ident_bf16[:])
+            nc.tensor.matmul(
+                out=n_row[:],
+                lhsT=n_halves[:, h : h + 1].to_broadcast([P, P]),
+                rhs=ident_f32[:],
+                start=(h == 0),
+                stop=(h == HALVES - 1),
+            )
             z_grouped = keep.tile([P, P, PACK], BF16, name="z_grouped%d" % h, align_bytes=64)
-            nc.vector.tensor_copy(out=z_grouped[:], in_=zt[:].rearrange("p t i -> p i t"))
+            nc.scalar.copy(out=z_grouped[:], in_=zt[:].rearrange("p t i -> p i t"))
+            cols = slice(h * P, (h + 1) * P)
             nc.vector.quantize_mx(
-                out=z_codes[:, h * P : (h + 1) * P].bitcast(FP8X4),
-                scales=z_scales[:, h * P : (h + 1) * P],
+                out=z_codes[:, cols].bitcast(FP8X4),
+                scales=z_scales[:, cols],
                 in_=z_grouped[:].rearrange("p i t -> p (i t)"),
             )
-        for h in range(HALVES):
             nc.tensor.matmul_mx(
                 out=gram[:],
-                lhsT=z_codes[:, h * P : (h + 1) * P].bitcast(FP8X4),
-                lhsT_scale=z_scales[:, h * P : (h + 1) * P],
-                rhs=z_codes[:, h * P : (h + 1) * P].bitcast(FP8X4),
-                rhs_scale=z_scales[:, h * P : (h + 1) * P],
+                lhsT=z_codes[:, cols].bitcast(FP8X4),
+                lhsT_scale=z_scales[:, cols],
+                rhs=z_codes[:, cols].bitcast(FP8X4),
+                rhs_scale=z_scales[:, cols],
                 start=(h == 0),
                 stop=(h == HALVES - 1),
             )
 
-        n = keep.tile([P, 1], F32)
-        nc.vector.tensor_add(out=n[:], in0=n_halves[:, 0:1], in1=n_halves[:, 1:2])
-        n_row = psum_tail.tile([P, P], F32)
-        nc.tensor.matmul(out=n_row[:], lhsT=n[:, 0:1].to_broadcast([P, P]), rhs=ident_f32[:], start=True, stop=True)
+        for g in range(WHOLE_GROUPS):
+            for h in range(HALVES):
+                z_pass(g, h)
+        for g in range(WHOLE_GROUPS, GROUPS):
+            z_pass(g, 0)
+        for g in range(WHOLE_GROUPS, GROUPS - 1):
+            z_pass(g, 1)
+        finish_bank(0)
+        z_pass(GROUPS - 1, 1)
+        finish_bank(1)
+
         n_sum = keep.tile([P, P], F32)
-        nc.vector.tensor_scalar(out=n_sum[:], in0=n_row[:], scalar1=n[:, 0:1], scalar2=None, op0=ALU.add)
+        nc.vector.tensor_scalar(
+            out=n_sum[:], in0=n_row[:], scalar1=n_halves[:, 0:1], scalar2=n_halves[:, 1:2], op0=ALU.add, op1=ALU.add
+        )
 
         sq = keep.tile([P, P], F32)
         nc.vector.scalar_tensor_tensor(

@@ -20,6 +20,7 @@ R = 1024
 GROUPS = D // K_PASS
 N_TILE = 512
 HALVES = R // N_TILE
+Z_PIECES = ((0, 512), (512, 256), (768, 256))
 PLANES = 4
 GROUPS_PER_X_LOAD = 8
 GROUPS_PER_W_LOAD = 2
@@ -64,8 +65,8 @@ def tile_metric_learning_based_adjacency_matrix_k_kernel(tc, features, P_words, 
                 in_=P_words[g0 : g0 + GROUPS_PER_W_LOAD].rearrange("g p n t -> p g (n t)").bitcast(I32),
             )
             for j in range(GROUPS_PER_W_LOAD):
-                for h in range(HALVES):
-                    w_words[(g0 + j, h)] = w_sb[:, j, h * N_TILE : (h + 1) * N_TILE]
+                for c, (first, width) in enumerate(Z_PIECES):
+                    w_words[(g0 + j, c)] = w_sb[:, j, first : first + width]
         w_first = keep.tile([P, SPLIT_GROUPS, N_TILE], U32, align_bytes=64)
         nc.sync.dma_start(
             out=w_first[:].bitcast(I32),
@@ -73,12 +74,23 @@ def tile_metric_learning_based_adjacency_matrix_k_kernel(tc, features, P_words, 
         )
         for g in range(WHOLE_GROUPS, GROUPS):
             w_words[(g, 0)] = w_first[:, g - WHOLE_GROUPS, :]
+        for g in range(WHOLE_GROUPS, GROUPS - 1):
             w_second = keep.tile([P, N_TILE], U32, name="w_second%d" % g, align_bytes=64)
             nc.sync.dma_start(
                 out=w_second[:].bitcast(I32),
                 in_=P_words[g, :, N_TILE:R, :].rearrange("p n t -> p (n t)").bitcast(I32),
             )
-            w_words[(g, 1)] = w_second[:]
+            for c in (1, 2):
+                first, width = Z_PIECES[c]
+                w_words[(g, c)] = w_second[:, first - N_TILE : first - N_TILE + width]
+        for c in (1, 2):
+            first, width = Z_PIECES[c]
+            w_last = keep.tile([P, width], U32, name="w_last%d" % c, align_bytes=64)
+            nc.sync.dma_start(
+                out=w_last[:].bitcast(I32),
+                in_=P_words[GROUPS - 1, :, first : first + width, :].rearrange("p n t -> p (n t)").bitcast(I32),
+            )
+            w_words[(GROUPS - 1, c)] = w_last[:]
 
         ident_f32 = keep.tile([P, P], F32)
         make_identity(nc, ident_f32[:])
@@ -94,6 +106,8 @@ def tile_metric_learning_based_adjacency_matrix_k_kernel(tc, features, P_words, 
         nc.gpsimd.memset(one[:], 1.0)
         sqrt_of_one = keep.tile([P, 1], F32)
         nc.scalar.activation(out=sqrt_of_one[:], in_=one[:], func=ACT.Sqrt)
+        pow_of_one = keep.tile([P, 1], F32)
+        nc.gpsimd.tensor_tensor(out=pow_of_one[:], in0=one[:], in1=minus_half[:], op=ALU.pow)
 
         x_codes = keep.tile([P, GROUPS * P], U32, align_bytes=64)
         x_scales = keep.tile([P, GROUPS * P], U8, align_bytes=64)
@@ -118,44 +132,59 @@ def tile_metric_learning_based_adjacency_matrix_k_kernel(tc, features, P_words, 
                 cols = slice(bank * GROUPS_PER_BANK * P, (bank + 1) * GROUPS_PER_BANK * P)
                 nc.vector.quantize_mx(out=x_codes[:, cols].bitcast(FP8X4), scales=x_scales[:, cols], in_=grouped[:])
 
-        z_banks = [psum_z.tile([P, N_TILE], F32, name="z%d" % h) for h in range(HALVES)]
+        z_banks = [psum_z.tile([P, width], F32, name="z%d" % c) for c, (first, width) in enumerate(Z_PIECES)]
 
-        def z_pass(g, h):
+        def z_pass(g, c):
             a, b = divmod(g, PLANES)
+            first, width = Z_PIECES[c]
             nc.tensor.matmul_mx(
-                out=z_banks[h][:],
+                out=z_banks[c][:],
                 lhsT=x_codes[:, g * P : (g + 1) * P].bitcast(FP8X4),
                 lhsT_scale=x_scales[:, g * P : (g + 1) * P],
-                rhs=w_words[(g, h)].bitcast(FP8X4),
-                rhs_scale=w_planes[4 * b : P, a * R + h * N_TILE : a * R + (h + 1) * N_TILE],
+                rhs=w_words[(g, c)].bitcast(FP8X4),
+                rhs_scale=w_planes[4 * b : P, a * R + first : a * R + first + width],
                 start=(g == 0),
                 stop=(g == GROUPS - 1),
             )
 
         psum_tail = ctx.enter_context(tc.psum_pool(name="psum_tail", bufs=1))
-        n_halves = keep.tile([P, HALVES], F32)
+        n_parts = keep.tile([P, len(Z_PIECES)], F32)
         z_codes = keep.tile([P, HALVES * P], U32, align_bytes=64)
         z_scales = keep.tile([P, HALVES * P], U8, align_bytes=64)
         gram = psum_tail.tile([P, P], F32)
         n_row = psum_tail.tile([P, P], F32)
 
-        def finish_bank(h):
-            z_sorted = keep.tile([P, PACK, P], BF16, name="z_sorted%d" % h)
-            nc.vector.tensor_copy(out=z_sorted[:], in_=z_banks[h][:].rearrange("i (p t) -> i t p", t=PACK))
-            z_squared = keep.tile([P, N_TILE], F32, name="z_squared%d" % h)
+        z_sorted = [keep.tile([P, PACK, P], BF16, name="z_sorted%d" % h) for h in range(HALVES)]
+
+        def empty_bank(c, copy_on_vector):
+            first, width = Z_PIECES[c]
+            h, inside = divmod(first, N_TILE)
+            sorted_piece = z_sorted[h][:, :, inside // PACK : (inside + width) // PACK]
+            bank_by_t = z_banks[c][:].rearrange("i (p t) -> i t p", t=PACK)
+            if copy_on_vector:
+                nc.vector.tensor_copy(out=sorted_piece, in_=bank_by_t)
+            else:
+                nc.scalar.copy(out=sorted_piece, in_=bank_by_t)
+            z_squared = keep.tile([P, width], F32, name="z_squared%d" % c)
             nc.scalar.activation(
-                out=z_squared[:], in_=z_banks[h][:], func=ACT.Square, accum_out=n_halves[:, h : h + 1]
+                out=z_squared[:], in_=z_banks[c][:], func=ACT.Square, accum_out=n_parts[:, c : c + 1]
             )
-            zt = psum_tail.tile([P, PACK, P], BF16, name="zt%d" % h)
-            for t in range(PACK):
-                nc.tensor.transpose(out=zt[:, t, :], in_=z_sorted[:, t, :], identity=ident_bf16[:])
+
+        def spread_n(c):
             nc.tensor.matmul(
                 out=n_row[:],
-                lhsT=n_halves[:, h : h + 1].to_broadcast([P, P]),
+                lhsT=n_parts[:, c : c + 1].to_broadcast([P, P]),
                 rhs=ident_f32[:],
-                start=(h == 0),
-                stop=(h == HALVES - 1),
+                start=(c == 0),
+                stop=(c == len(Z_PIECES) - 1),
             )
+
+        def close_half(h, banks):
+            zt = psum_tail.tile([P, PACK, P], BF16, name="zt%d" % h)
+            for t in range(PACK):
+                nc.tensor.transpose(out=zt[:, t, :], in_=z_sorted[h][:, t, :], identity=ident_bf16[:])
+            for c in banks:
+                spread_n(c)
             z_grouped = keep.tile([P, P, PACK], BF16, name="z_grouped%d" % h, align_bytes=64)
             nc.scalar.copy(out=z_grouped[:], in_=zt[:].rearrange("p t i -> p i t"))
             cols = slice(h * P, (h + 1) * P)
@@ -175,19 +204,26 @@ def tile_metric_learning_based_adjacency_matrix_k_kernel(tc, features, P_words, 
             )
 
         for g in range(WHOLE_GROUPS):
-            for h in range(HALVES):
-                z_pass(g, h)
+            for c in range(len(Z_PIECES)):
+                z_pass(g, c)
         for g in range(WHOLE_GROUPS, GROUPS):
             z_pass(g, 0)
         for g in range(WHOLE_GROUPS, GROUPS - 1):
             z_pass(g, 1)
-        finish_bank(0)
+            z_pass(g, 2)
+        empty_bank(0, True)
+        close_half(0, (0,))
         z_pass(GROUPS - 1, 1)
-        finish_bank(1)
+        empty_bank(1, False)
+        z_pass(GROUPS - 1, 2)
+        empty_bank(2, True)
+        close_half(1, (1, 2))
 
+        n_early = keep.tile([P, 1], F32)
+        nc.vector.tensor_add(out=n_early[:], in0=n_parts[:, 0:1], in1=n_parts[:, 1:2])
         n_sum = keep.tile([P, P], F32)
         nc.vector.tensor_scalar(
-            out=n_sum[:], in0=n_row[:], scalar1=n_halves[:, 0:1], scalar2=n_halves[:, 1:2], op0=ALU.add, op1=ALU.add
+            out=n_sum[:], in0=n_row[:], scalar1=n_early[:, 0:1], scalar2=n_parts[:, 2:3], op0=ALU.add, op1=ALU.add
         )
 
         sq = keep.tile([P, P], F32)
@@ -210,9 +246,7 @@ def tile_metric_learning_based_adjacency_matrix_k_kernel(tc, features, P_words, 
         inv_sqrt_deg = keep.tile([P, 1], F32)
         nc.gpsimd.tensor_tensor(out=inv_sqrt_deg[:], in0=deg[:], in1=minus_half[:], op=ALU.pow)
         inv_row = psum_tail.tile([P, P], F32)
-        nc.tensor.matmul(
-            out=inv_row[:], lhsT=inv_sqrt_deg[:, 0:1].to_broadcast([P, P]), rhs=ident_f32[:], start=True, stop=True
-        )
+        nc.tensor.transpose(out=inv_row[:], in_=inv_sqrt_deg[:, 0:1].to_broadcast([P, P]), identity=ident_f32[:])
         normalized = keep.tile([P, P], F32)
         nc.vector.scalar_tensor_tensor(
             out=normalized[:], in0=adjacency[:], scalar=inv_sqrt_deg[:, 0:1], in1=inv_row[:], op0=ALU.mult, op1=ALU.mult

@@ -106,8 +106,6 @@ def tile_metric_learning_based_adjacency_matrix_k_kernel(tc, features, P_words, 
         nc.gpsimd.memset(one[:], 1.0)
         sqrt_of_one = keep.tile([P, 1], F32)
         nc.scalar.activation(out=sqrt_of_one[:], in_=one[:], func=ACT.Sqrt)
-        pow_of_one = keep.tile([P, 1], F32)
-        nc.gpsimd.tensor_tensor(out=pow_of_one[:], in0=one[:], in1=minus_half[:], op=ALU.pow)
 
         x_codes = keep.tile([P, GROUPS * P], U32, align_bytes=64)
         x_scales = keep.tile([P, GROUPS * P], U8, align_bytes=64)

@@ -29,7 +29,9 @@ SPLIT_GROUPS = 4
 WHOLE_GROUPS = GROUPS - SPLIT_GROUPS
 
 SQ_MIN = 2.0 ** -100
-SQ_MAX = 2.0 ** 118
+ROOT_SCALE = 2.0 ** -6
+ROOT_MAX = 2.0 ** 60
+SQ_HUGE = 2.0 ** 126
 
 FLOPS = 2 * P * D * R + 2 * P * P * R
 
@@ -100,6 +102,8 @@ def tile_metric_learning_based_adjacency_matrix_k_kernel(tc, features, P_words, 
         nc.vector.tensor_scalar(
             out=off_diagonal[:], in0=ident_f32[:], scalar1=-1.0, scalar2=1.0, op0=ALU.mult, op1=ALU.add
         )
+        twice_on_diagonal = keep.tile([P, P], F32)
+        nc.vector.tensor_scalar_add(out=twice_on_diagonal[:], in0=ident_f32[:], scalar1=1.0)
         minus_half = keep.tile([P, 1], F32)
         nc.gpsimd.memset(minus_half[:], -0.5)
         one = keep.tile([P, 1], F32)
@@ -224,21 +228,32 @@ def tile_metric_learning_based_adjacency_matrix_k_kernel(tc, features, P_words, 
             out=n_sum[:], in0=n_row[:], scalar1=n_early[:, 0:1], scalar2=n_parts[:, 2:3], op0=ALU.add, op1=ALU.add
         )
 
+        n_sum_safe = keep.tile([P, P], F32)
+        nc.vector.tensor_mul(out=n_sum_safe[:], in0=n_sum[:], in1=twice_on_diagonal[:])
+
         sq = keep.tile([P, P], F32)
         nc.vector.scalar_tensor_tensor(
-            out=sq[:], in0=gram[:], scalar=-2.0, in1=n_sum[:], op0=ALU.mult, op1=ALU.add
-        )
-        sq_clamped = keep.tile([P, P], F32)
-        nc.vector.tensor_scalar(
-            out=sq_clamped[:], in0=sq[:], scalar1=SQ_MIN, scalar2=SQ_MAX, op0=ALU.max, op1=ALU.min
+            out=sq[:], in0=gram[:], scalar=-2.0, in1=n_sum_safe[:], op0=ALU.mult, op1=ALU.add
         )
         root = keep.tile([P, P], F32)
-        nc.scalar.activation(out=root[:], in_=sq_clamped[:], func=ACT.Sqrt)
+        nc.scalar.activation(out=root[:], in_=sq[:], func=ACT.Sqrt, scale=ROOT_SCALE * ROOT_SCALE)
+        keep_root = keep.tile([P, P], F32)
+        nc.vector.scalar_tensor_tensor(
+            out=keep_root[:], in0=sq[:], scalar=SQ_MIN, in1=off_diagonal[:], op0=ALU.is_ge, op1=ALU.mult
+        )
+        root_floor = keep.tile([P, P], F32)
+        nc.vector.tensor_scalar(
+            out=root_floor[:], in0=sq[:], scalar1=SQ_HUGE, scalar2=ROOT_MAX, op0=ALU.is_ge, op1=ALU.mult
+        )
+        root_bounded = keep.tile([P, P], F32)
+        nc.vector.scalar_tensor_tensor(
+            out=root_bounded[:], in0=root[:], scalar=ROOT_MAX, in1=root_floor[:], op0=ALU.min, op1=ALU.max
+        )
         dist = keep.tile([P, P], F32)
-        nc.vector.tensor_mul(out=dist[:], in0=root[:], in1=off_diagonal[:])
+        nc.vector.tensor_mul(out=dist[:], in0=root_bounded[:], in1=keep_root[:])
         adjacency = keep.tile([P, P], F32)
         deg = keep.tile([P, 1], F32)
-        nc.scalar.activation(out=adjacency[:], in_=dist[:], func=ACT.Exp, scale=-1.0, accum_out=deg[:])
+        nc.scalar.activation(out=adjacency[:], in_=dist[:], func=ACT.Exp, scale=-1.0 / ROOT_SCALE, accum_out=deg[:])
         nc.sync.dma_start(out=out_1[:, :], in_=adjacency[:])
 
         inv_sqrt_deg = keep.tile([P, 1], F32)

from contextlib import ExitStack

import concourse.mybir as mybir
from concourse.masks import make_identity

F32 = mybir.dt.float32
BF16 = mybir.dt.bfloat16
I32 = mybir.dt.int32
U32 = mybir.dt.uint32
U8 = mybir.dt.uint8
FP8X4 = mybir.dt.float8_e4m3fn_x4
ALU = mybir.AluOpType
ACT = mybir.ActivationFunctionType

P = 128
PACK = 4
K_PASS = P * PACK
D = 16384
R = 1024
GROUPS = D // K_PASS
N_TILE = 512
HALVES = R // N_TILE
Z_PIECES = ((0, 512), (512, 256), (768, 256))
PLANES = 4
GROUPS_PER_X_LOAD = 8
GROUPS_PER_W_LOAD = 2
GROUPS_PER_BANK = 2
SPLIT_GROUPS = 4
WHOLE_GROUPS = GROUPS - SPLIT_GROUPS

SQ_MIN = 2.0 ** -100
ROOT_SCALE = 2.0 ** -6
ROOT_MAX = 2.0 ** 60
SQ_HUGE = 2.0 ** 126

FLOPS = 2 * P * D * R + 2 * P * P * R


def tile_metric_learning_based_adjacency_matrix_k_kernel(tc, features, P_words, P_scales, out_0, out_1):
    nc = tc.nc
    with ExitStack() as ctx:
        keep = ctx.enter_context(tc.tile_pool(name="keep", bufs=1))
        stage = ctx.enter_context(tc.tile_pool(name="stage", bufs=4))
        psum_z = ctx.enter_context(tc.psum_pool(name="psum_z", bufs=1))

        x_loads = []
        for c in range(GROUPS // GROUPS_PER_X_LOAD):
            x_sb = keep.tile([P, GROUPS_PER_X_LOAD * K_PASS], BF16, name="x%d" % c)
            width = GROUPS_PER_X_LOAD * K_PASS
            nc.sync.dma_start(out=x_sb[:], in_=features[:, c * width : (c + 1) * width])
            x_loads.append(x_sb)

        w_planes = keep.tile([P, (GROUPS // PLANES) * R], U8, align_bytes=64)
        nc.vector.memset(w_planes[:].bitcast(I32), 0)
        for a in range(GROUPS // PLANES):
            for q in range(4):
                nc.sync.dma_start(
                    out=w_planes[32 * q : 32 * q + 16, a * R : (a + 1) * R].bitcast(I32),
                    in_=P_scales[PLANES * a : PLANES * (a + 1), 4 * q : 4 * q + 4, :].bitcast(I32),
                )

        w_words = {}
        for g0 in range(0, WHOLE_GROUPS, GROUPS_PER_W_LOAD):
            w_sb = keep.tile([P, GROUPS_PER_W_LOAD, R], U32, name="w%d" % g0, align_bytes=64)
            nc.sync.dma_start(
                out=w_sb[:].bitcast(I32),
                in_=P_words[g0 : g0 + GROUPS_PER_W_LOAD].rearrange("g p n t -> p g (n t)").bitcast(I32),
            )
            for j in range(GROUPS_PER_W_LOAD):
                for c, (first, width) in enumerate(Z_PIECES):
                    w_words[(g0 + j, c)] = w_sb[:, j, first : first + width]
        w_first = keep.tile([P, SPLIT_GROUPS, N_TILE], U32, align_bytes=64)
        nc.sync.dma_start(
            out=w_first[:].bitcast(I32),
            in_=P_words[WHOLE_GROUPS:GROUPS, :, 0:N_TILE, :].rearrange("g p n t -> p g (n t)").bitcast(I32),
        )
        for g in range(WHOLE_GROUPS, GROUPS):
            w_words[(g, 0)] = w_first[:, g - WHOLE_GROUPS, :]
        for g in range(WHOLE_GROUPS, GROUPS - 1):
            w_second = keep.tile([P, N_TILE], U32, name="w_second%d" % g, align_bytes=64)
            nc.sync.dma_start(
                out=w_second[:].bitcast(I32),
                in_=P_words[g, :, N_TILE:R, :].rearrange("p n t -> p (n t)").bitcast(I32),
            )
            for c in (1, 2):
                first, width = Z_PIECES[c]
                w_words[(g, c)] = w_second[:, first - N_TILE : first - N_TILE + width]
        for c in (1, 2):
            first, width = Z_PIECES[c]
            w_last = keep.tile([P, width], U32, name="w_last%d" % c, align_bytes=64)
            nc.sync.dma_start(
                out=w_last[:].bitcast(I32),
                in_=P_words[GROUPS - 1, :, first : first + width, :].rearrange("p n t -> p (n t)").bitcast(I32),
            )
            w_words[(GROUPS - 1, c)] = w_last[:]

        ident_f32 = keep.tile([P, P], F32)
        make_identity(nc, ident_f32[:])
        ident_bf16 = keep.tile([P, P], BF16)
        make_identity(nc, ident_bf16[:])
        off_diagonal = keep.tile([P, P], F32)
        nc.vector.tensor_scalar(
            out=off_diagonal[:], in0=ident_f32[:], scalar1=-1.0, scalar2=1.0, op0=ALU.mult, op1=ALU.add
        )
        twice_on_diagonal = keep.tile([P, P], F32)
        nc.vector.tensor_scalar_add(out=twice_on_diagonal[:], in0=ident_f32[:], scalar1=1.0)
        minus_half = keep.tile([P, 1], F32)
        nc.gpsimd.memset(minus_half[:], -0.5)
        one = keep.tile([P, 1], F32)
        nc.gpsimd.memset(one[:], 1.0)
        sqrt_of_one = keep.tile([P, 1], F32)
        nc.scalar.activation(out=sqrt_of_one[:], in_=one[:], func=ACT.Sqrt)

        x_codes = keep.tile([P, GROUPS * P], U32, align_bytes=64)
        x_scales = keep.tile([P, GROUPS * P], U8, align_bytes=64)
        with tc.psum_pool(name="psum_x", bufs=4) as psum_x:
            for bank in range(GROUPS // GROUPS_PER_BANK):
                xt = psum_x.tile([P, GROUPS_PER_BANK, 2, P], F32)
                for j in range(GROUPS_PER_BANK):
                    g = bank * GROUPS_PER_BANK + j
                    x_words = x_loads[g // GROUPS_PER_X_LOAD][:].bitcast(F32)
                    first = (g % GROUPS_PER_X_LOAD) * (K_PASS // 2)
                    for u in range(2):
                        nc.tensor.transpose(
                            out=xt[:, j, u, :],
                            in_=x_words[:, first + u : first + K_PASS // 2 : 2],
                            identity=ident_f32[:],
                        )
                grouped = stage.tile([P, GROUPS_PER_BANK * K_PASS], BF16, align_bytes=64)
                nc.scalar.copy(
                    out=grouped[:].bitcast(F32).rearrange("p (j i u) -> p j i u", j=GROUPS_PER_BANK, u=2),
                    in_=xt[:].rearrange("p j u i -> p j i u"),
                )
                cols = slice(bank * GROUPS_PER_BANK * P, (bank + 1) * GROUPS_PER_BANK * P)
                nc.vector.quantize_mx(out=x_codes[:, cols].bitcast(FP8X4), scales=x_scales[:, cols], in_=grouped[:])

        z_banks = [psum_z.tile([P, width], F32, name="z%d" % c) for c, (first, width) in enumerate(Z_PIECES)]

        def z_pass(g, c):
            a, b = divmod(g, PLANES)
            first, width = Z_PIECES[c]
            nc.tensor.matmul_mx(
                out=z_banks[c][:],
                lhsT=x_codes[:, g * P : (g + 1) * P].bitcast(FP8X4),
                lhsT_scale=x_scales[:, g * P : (g + 1) * P],
                rhs=w_words[(g, c)].bitcast(FP8X4),
                rhs_scale=w_planes[4 * b : P, a * R + first : a * R + first + width],
                start=(g == 0),
                stop=(g == GROUPS - 1),
            )

        psum_tail = ctx.enter_context(tc.psum_pool(name="psum_tail", bufs=1))
        n_parts = keep.tile([P, len(Z_PIECES)], F32)
        z_codes = keep.tile([P, HALVES * P], U32, align_bytes=64)
        z_scales = keep.tile([P, HALVES * P], U8, align_bytes=64)
        gram = psum_tail.tile([P, P], F32)
        n_row = psum_tail.tile([P, P], F32)

        z_sorted = [keep.tile([P, PACK, P], BF16, name="z_sorted%d" % h) for h in range(HALVES)]

        def empty_bank(c, copy_on_vector):
            first, width = Z_PIECES[c]
            h, inside = divmod(first, N_TILE)
            sorted_piece = z_sorted[h][:, :, inside // PACK : (inside + width) // PACK]
            bank_by_t = z_banks[c][:].rearrange("i (p t) -> i t p", t=PACK)
            if copy_on_vector:
                nc.vector.tensor_copy(out=sorted_piece, in_=bank_by_t)
            else:
                nc.scalar.copy(out=sorted_piece, in_=bank_by_t)
            z_squared = keep.tile([P, width], F32, name="z_squared%d" % c)
            nc.scalar.activation(
                out=z_squared[:], in_=z_banks[c][:], func=ACT.Square, accum_out=n_parts[:, c : c + 1]
            )

        def spread_n(c):
            nc.tensor.matmul(
                out=n_row[:],
                lhsT=n_parts[:, c : c + 1].to_broadcast([P, P]),
                rhs=ident_f32[:],
                start=(c == 0),
                stop=(c == len(Z_PIECES) - 1),
            )

        def close_half(h, banks):
            zt = psum_tail.tile([P, PACK, P], BF16, name="zt%d" % h)
            for t in range(PACK):
                nc.tensor.transpose(out=zt[:, t, :], in_=z_sorted[h][:, t, :], identity=ident_bf16[:])
            for c in banks:
                spread_n(c)
            z_grouped = keep.tile([P, P, PACK], BF16, name="z_grouped%d" % h, align_bytes=64)
            nc.scalar.copy(out=z_grouped[:], in_=zt[:].rearrange("p t i -> p i t"))
            cols = slice(h * P, (h + 1) * P)
            nc.vector.quantize_mx(
                out=z_codes[:, cols].bitcast(FP8X4),
                scales=z_scales[:, cols],
                in_=z_grouped[:].rearrange("p i t -> p (i t)"),
            )
            nc.tensor.matmul_mx(
                out=gram[:],
                lhsT=z_codes[:, cols].bitcast(FP8X4),
                lhsT_scale=z_scales[:, cols],
                rhs=z_codes[:, cols].bitcast(FP8X4),
                rhs_scale=z_scales[:, cols],
                start=(h == 0),
                stop=(h == HALVES - 1),
            )

        for g in range(WHOLE_GROUPS):
            for c in range(len(Z_PIECES)):
                z_pass(g, c)
        for g in range(WHOLE_GROUPS, GROUPS):
            z_pass(g, 0)
        for g in range(WHOLE_GROUPS, GROUPS - 1):
            z_pass(g, 1)
            z_pass(g, 2)
        empty_bank(0, True)
        close_half(0, (0,))
        z_pass(GROUPS - 1, 1)
        empty_bank(1, False)
        z_pass(GROUPS - 1, 2)
        empty_bank(2, True)
        close_half(1, (1, 2))

        n_early = keep.tile([P, 1], F32)
        nc.vector.tensor_add(out=n_early[:], in0=n_parts[:, 0:1], in1=n_parts[:, 1:2])
        n_sum = keep.tile([P, P], F32)
        nc.vector.tensor_scalar(
            out=n_sum[:], in0=n_row[:], scalar1=n_early[:, 0:1], scalar2=n_parts[:, 2:3], op0=ALU.add, op1=ALU.add
        )

        n_sum_safe = keep.tile([P, P], F32)
        nc.vector.tensor_mul(out=n_sum_safe[:], in0=n_sum[:], in1=twice_on_diagonal[:])

        sq = keep.tile([P, P], F32)
        nc.vector.scalar_tensor_tensor(
            out=sq[:], in0=gram[:], scalar=-2.0, in1=n_sum_safe[:], op0=ALU.mult, op1=ALU.add
        )
        root = keep.tile([P, P], F32)
        nc.scalar.activation(out=root[:], in_=sq[:], func=ACT.Sqrt, scale=ROOT_SCALE * ROOT_SCALE)
        keep_root = keep.tile([P, P], F32)
        nc.vector.scalar_tensor_tensor(
            out=keep_root[:], in0=sq[:], scalar=SQ_MIN, in1=off_diagonal[:], op0=ALU.is_ge, op1=ALU.mult
        )
        root_floor = keep.tile([P, P], F32)
        nc.vector.tensor_scalar(
            out=root_floor[:], in0=sq[:], scalar1=SQ_HUGE, scalar2=ROOT_MAX, op0=ALU.is_ge, op1=ALU.mult
        )
        root_bounded = keep.tile([P, P], F32)
        nc.vector.scalar_tensor_tensor(
            out=root_bounded[:], in0=root[:], scalar=ROOT_MAX, in1=root_floor[:], op0=ALU.min, op1=ALU.max
        )
        dist = keep.tile([P, P], F32)
        nc.vector.tensor_mul(out=dist[:], in0=root_bounded[:], in1=keep_root[:])
        adjacency = keep.tile([P, P], F32)
        deg = keep.tile([P, 1], F32)
        nc.scalar.activation(out=adjacency[:], in_=dist[:], func=ACT.Exp, scale=-1.0 / ROOT_SCALE, accum_out=deg[:])
        nc.sync.dma_start(out=out_1[:, :], in_=adjacency[:])

        inv_sqrt_deg = keep.tile([P, 1], F32)
        nc.gpsimd.tensor_tensor(out=inv_sqrt_deg[:], in0=deg[:], in1=minus_half[:], op=ALU.pow)
        inv_row = psum_tail.tile([P, P], F32)
        nc.tensor.transpose(out=inv_row[:], in_=inv_sqrt_deg[:, 0:1].to_broadcast([P, P]), identity=ident_f32[:])
        normalized = keep.tile([P, P], F32)
        nc.vector.scalar_tensor_tensor(
            out=normalized[:], in0=adjacency[:], scalar=inv_sqrt_deg[:, 0:1], in1=inv_row[:], op0=ALU.mult, op1=ALU.mult
        )
        nc.sync.dma_start(out=out_0[:, :], in_=normalized[:])
